import numpy as np
import ml_dtypes


def mxq(x, axis, fmt="e4m3"):
    dtype, down = {"e4m3": (ml_dtypes.float8_e4m3fn, 7), "e5m2": (ml_dtypes.float8_e5m2, 14)}[fmt]
    v = np.moveaxis(np.asarray(x, np.float32).astype(ml_dtypes.bfloat16).astype(np.float64), axis, -1)
    blocks = v.reshape(v.shape[:-1] + (-1, 32))
    amax = np.abs(blocks).max(-1, keepdims=True)
    byte = np.maximum(np.where(amax > 0, np.frexp(amax)[1] - 1 + 127, 0) - down, 1)
    scale = np.exp2(byte - 127.0)
    codes = (blocks / scale).astype(np.float32).astype(dtype).astype(np.float64)
    return np.moveaxis((codes * scale).reshape(v.shape), -1, axis)


WIDE = False


def mx_kscale(k):
    if not WIDE:
        return np.ones(k)
    levels = np.array([20, -20, 10, -10, 0])
    a = np.random.permutation(np.resize(levels, k // 512 * 4)).reshape(k // 512, 4)
    idx = np.arange(k)
    return np.exp2(a[idx // 512, idx % 128 // 32])


BF16 = ml_dtypes.bfloat16


def bf(x):
    return np.asarray(x, np.float32).astype(BF16)


def f64(x):
    return np.asarray(x).astype(np.float64)


B, S, D, E, R = 4, 1024, 1024, 8, 64
K = E * R


def setup_inputs():
    u = mx_kscale(K).reshape(E, R)
    x = np.random.standard_normal((B, S, D))
    W = np.random.standard_normal((E, R, D)) * (1.0 / np.sqrt(D)) / u[:, :, None]
    g = (np.random.standard_normal((E, B, S, R))
         * np.exp2(np.random.randint(-12, 1, (1, B, S, 1))) * 4.0 * u[:, None, None, :])
    return {"x": bf(x), "W": bf(W), "grad_out": bf(g)}


def reference(x, W, grad_out):
    g2 = f64(grad_out).transpose(1, 2, 0, 3).reshape(B * S, K)
    w2 = f64(W).reshape(K, D)
    gx = mxq(g2, 1, "e5m2") @ mxq(w2, 0, "e4m3")
    return gx.reshape(B, S, D)

@@ -1,0 +1,181 @@
+from contextlib import ExitStack
+
+import concourse.mybir as mybir
+from concourse.masks import make_identity
+
+F32 = mybir.dt.float32
+BF16 = mybir.dt.bfloat16
+U32 = mybir.dt.uint32
+U8 = mybir.dt.uint8
+E4M3X4 = mybir.dt.float8_e4m3fn_x4
+E5M2X4 = mybir.dt.float8_e5m2_x4
+
+P = 128
+E, R, D = 8, 64, 1024
+K = E * R
+TOKENS = 4096
+NT = TOKENS // P
+GROUP = 4
+NG = NT // GROUP
+N_TILE = 512
+CHUNKS = (8, 8, 16)
+W_SPLIT = 672
+VECTOR_BANKS = (1, 6)
+HALF_STORES = 1
+MANUAL = False
+
+FLOPS = 2 * TOKENS * K * D
+BYTES = TOKENS * K * 2 + K * D * 2 + TOKENS * D * 4
+
+
+def tile_moelineara_t_kernel(tc, x, W, grad_out, out):
+    nc = tc.nc
+    gv = grad_out.rearrange("e b (c t) r -> (b c) e (t r)", t=NT)
+    wv = W.rearrange("e (q j) d -> (e q) (j d)", j=4)
+    ov = out.rearrange("b (c t) d -> (b c) (t d)", t=NT)
+
+    with ExitStack() as ctx:
+        keep = ctx.enter_context(tc.tile_pool(name="keep", bufs=1))
+        ring = ctx.enter_context(tc.tile_pool(name="ring", bufs=3))
+        stages = ctx.enter_context(tc.tile_pool(name="stages", bufs=6))
+        tpsum = ctx.enter_context(tc.psum_pool(name="tpsum", bufs=2))
+        apsum = ctx.enter_context(tc.psum_pool(name="apsum", bufs=6))
+        if MANUAL:
+            ctx.enter_context(tc.manual_schedule())
+
+        wraw = keep.tile([P, 4, D], BF16, name="wraw")
+        nc.sync.dma_start(out=wraw[:].rearrange("p j d -> p (j d)"), in_=wv)
+        raw = []
+        where = []
+        t_at = 0
+        for c, n in enumerate(CHUNKS):
+            chunk = keep.tile([P, E, n * R], BF16, name="raw%d" % c)
+            for h in range(2):
+                nc.sync.dma_start(
+                    out=chunk[:, 4 * h : 4 * h + 4, :],
+                    in_=gv[:, 4 * h : 4 * h + 4, t_at * R : (t_at + n) * R],
+                )
+            raw.append(chunk)
+            for t0 in range(0, n, GROUP):
+                where.append((c, t0))
+            t_at += n
+
+        ident = keep.tile([P, P], F32, name="ident")
+        make_identity(nc, ident[:])
+
+        wgrp = keep.tile([P, D, 4], BF16, name="wgrp", align_bytes=64)
+        wcodes = keep.tile([P, D], U32, name="wcodes", align_bytes=64)
+        wscales = keep.tile([P, D], U8, name="wscales", align_bytes=64)
+        nc.vector.tensor_copy(
+            out=wgrp[:, 0:W_SPLIT, :].rearrange("p (c i) j -> p c j i", i=4),
+            in_=wraw[:, :, 0:W_SPLIT].rearrange("p j (c i) -> p c j i", i=4),
+        )
+        nc.scalar.copy(
+            out=wgrp[:, W_SPLIT:D, :].rearrange("p (c i) j -> p c j i", i=4),
+            in_=wraw[:, :, W_SPLIT:D].rearrange("p j (c i) -> p c j i", i=4),
+        )
+        for n in range(D // N_TILE):
+            cols = slice(n * N_TILE, (n + 1) * N_TILE)
+            nc.vector.quantize_mx(
+                out=wcodes[:, cols].bitcast(E4M3X4),
+                scales=wscales[:, cols],
+                in_=wgrp[:, cols, :].rearrange("p c j -> p (c j)"),
+            )
+
+        gl_t = {}
+        xt_t = {}
+        gq_t = {}
+        code_t = {}
+        stage_t = {}
+
+        def relay(i):
+            if i < 0 or i >= NG:
+                return
+            c, t0 = where[i]
+            gl = ring.tile([P, GROUP * K], BF16, name="gl")
+            nc.vector.tensor_copy(
+                out=gl[:].rearrange("a (t e r) -> a t e r", t=GROUP, e=E),
+                in_=raw[c][:, :, t0 * R : (t0 + GROUP) * R].rearrange("a e (t r) -> a t e r", r=R),
+            )
+            gl_t[i] = gl
+
+        def transposes(i, h):
+            if i < 0 or i >= NG:
+                return
+            xt = tpsum.tile([P, 4, P], F32, name="xt")
+            words = gl_t[i][:].bitcast(F32).rearrange("a (t p u) -> a t u p", t=GROUP, u=2)
+            for tt in range(2):
+                for u in range(2):
+                    nc.tensor.transpose(xt[:, 2 * tt + u, :], words[:, 2 * h + tt, u, :], ident[:])
+            xt_t[(i, h)] = xt
+
+        def unload(i, h, on_scalar):
+            if i < 0 or i >= NG:
+                return
+            if h == 0:
+                gq = ring.tile([P, GROUP * K], BF16, name="gq", align_bytes=64)
+                gq_t[i] = gq
+            dst = gq_t[i][:].bitcast(F32).rearrange("p (t a u) -> p t a u", t=GROUP, u=2)
+            src = xt_t[(i, h)][:].rearrange("p (t u) a -> p t a u", u=2)
+            if on_scalar:
+                nc.scalar.copy(out=dst[:, 2 * h : 2 * h + 2], in_=src)
+            else:
+                nc.vector.tensor_copy(out=dst[:, 2 * h : 2 * h + 2], in_=src)
+
+        def quantise(i):
+            if i < 0 or i >= NG:
+                return
+            codes = ring.tile([P, GROUP * P], U32, name="gcodes", align_bytes=64)
+            scales = ring.tile([P, GROUP * P], U8, name="gscales", align_bytes=64)
+            nc.vector.quantize_mx(out=codes[:].bitcast(E5M2X4), scales=scales[:], in_=gq_t[i][:])
+            code_t[i] = (codes, scales)
+
+        def multiply(i, j_list):
+            if i < 0 or i >= NG:
+                return
+            codes, scales = code_t[i]
+            if i not in stage_t:
+                stage = stages.tile([P, GROUP, D], F32, name="stage")
+                stage_t[i] = stage
+            for j in j_list:
+                t, n = j // 2, j % 2
+                acc = apsum.tile([P, N_TILE], F32, name="acc")
+                nc.tensor.matmul_mx(
+                    out=acc[:],
+                    lhsT=codes[:, t * P : (t + 1) * P].bitcast(E5M2X4),
+                    lhsT_scale=scales[:, t * P : (t + 1) * P],
+                    rhs=wcodes[:, n * N_TILE : (n + 1) * N_TILE].bitcast(E4M3X4),
+                    rhs_scale=wscales[:, n * N_TILE : (n + 1) * N_TILE],
+                    start=True,
+                    stop=True,
+                )
+                dst = stage_t[i][:, t, n * N_TILE : (n + 1) * N_TILE]
+                if j in VECTOR_BANKS:
+                    nc.vector.tensor_copy(out=dst, in_=acc[:])
+                else:
+                    nc.scalar.copy(out=dst, in_=acc[:])
+
+        def store(i, t0, t1):
+            if i < 0 or i >= NG:
+                return
+            nc.sync.dma_start(
+                out=ov[:, (i * GROUP + t0) * D : (i * GROUP + t1) * D],
+                in_=stage_t[i][:, t0:t1, :].rearrange("p t d -> p (t d)"),
+            )
+
+        relay(0)
+        for i in range(-2, NG):
+            unload(i + 1, 1, i < 0)
+            multiply(i, (0, 1, 2, 3))
+            if i < HALF_STORES:
+                store(i, 0, 2)
+            quantise(i + 1)
+            transposes(i + 2, 0)
+            unload(i + 2, 0, i < 0)
+            relay(i + 3)
+            multiply(i, (4, 5, 6, 7))
+            transposes(i + 2, 1)
+            if i < HALF_STORES:
+                store(i, 2, 4)
+            else:
+                store(i, 0, 4)

@@ -21,7 +21,7 @@ N_TILE = 512
 CHUNKS = (8, 8, 16)
 W_SPLIT = 672
 VECTOR_BANKS = (1, 6)
-HALF_STORES = 1
+HALF_STORES = 8
 MANUAL = False
 
 FLOPS = 2 * TOKENS * K * D

@@ -15,14 +15,16 @@ E, R, D = 8, 64, 1024
 K = E * R
 TOKENS = 4096
 NT = TOKENS // P
-GROUP = 4
-NG = NT // GROUP
+PAIR = 2
+NU = NT // PAIR
 N_TILE = 512
 CHUNKS = (8, 8, 16)
 W_SPLIT = 672
-VECTOR_BANKS = (1, 6)
-HALF_STORES = 8
-MANUAL = False
+W_STEP = -2
+SCALAR_UNLOADS = 2
+TILE_STORES = 2
+AHEAD_RELAY, AHEAD_TRANSPOSE, AHEAD_UNLOAD, AHEAD_QUANTISE = 5, 4, 3, 2
+MANUAL = True
 
 FLOPS = 2 * TOKENS * K * D
 BYTES = TOKENS * K * 2 + K * D * 2 + TOKENS * D * 4
@@ -37,26 +39,28 @@ def tile_moelineara_t_kernel(tc, x, W, grad_out, out):
     with ExitStack() as ctx:
         keep = ctx.enter_context(tc.tile_pool(name="keep", bufs=1))
         ring = ctx.enter_context(tc.tile_pool(name="ring", bufs=3))
-        stages = ctx.enter_context(tc.tile_pool(name="stages", bufs=6))
+        stages = ctx.enter_context(tc.tile_pool(name="stages", bufs=NU))
         tpsum = ctx.enter_context(tc.psum_pool(name="tpsum", bufs=2))
         apsum = ctx.enter_context(tc.psum_pool(name="apsum", bufs=6))
         if MANUAL:
             ctx.enter_context(tc.manual_schedule())
 
         wraw = keep.tile([P, 4, D], BF16, name="wraw")
-        nc.sync.dma_start(out=wraw[:].rearrange("p j d -> p (j d)"), in_=wv)
-        raw = []
+        raw_words = []
         where = []
         t_at = 0
         for c, n in enumerate(CHUNKS):
-            chunk = keep.tile([P, E, n * R], BF16, name="raw%d" % c)
+            chunk = keep.tile([P, E * n * R], BF16, name="raw%d" % c)
+            by_expert = chunk[:].rearrange("a (e x) -> a e x", e=E)
             for h in range(2):
                 nc.sync.dma_start(
-                    out=chunk[:, 4 * h : 4 * h + 4, :],
+                    out=by_expert[:, 4 * h : 4 * h + 4, :],
                     in_=gv[:, 4 * h : 4 * h + 4, t_at * R : (t_at + n) * R],
                 )
-            raw.append(chunk)
-            for t0 in range(0, n, GROUP):
+            if c == 0:
+                nc.sync.dma_start(out=wraw[:].rearrange("p j d -> p (j d)"), in_=wv)
+            raw_words.append(chunk[:].bitcast(F32).rearrange("a (e t w u) -> a e t w u", e=E, w=R // 4, u=2))
+            for t0 in range(0, n, PAIR):
                 where.append((c, t0))
             t_at += n
 
@@ -66,21 +70,23 @@ def tile_moelineara_t_kernel(tc, x, W, grad_out, out):
         wgrp = keep.tile([P, D, 4], BF16, name="wgrp", align_bytes=64)
         wcodes = keep.tile([P, D], U32, name="wcodes", align_bytes=64)
         wscales = keep.tile([P, D], U8, name="wscales", align_bytes=64)
-        nc.vector.tensor_copy(
-            out=wgrp[:, 0:W_SPLIT, :].rearrange("p (c i) j -> p c j i", i=4),
-            in_=wraw[:, :, 0:W_SPLIT].rearrange("p j (c i) -> p c j i", i=4),
-        )
-        nc.scalar.copy(
-            out=wgrp[:, W_SPLIT:D, :].rearrange("p (c i) j -> p c j i", i=4),
-            in_=wraw[:, :, W_SPLIT:D].rearrange("p j (c i) -> p c j i", i=4),
-        )
-        for n in range(D // N_TILE):
-            cols = slice(n * N_TILE, (n + 1) * N_TILE)
-            nc.vector.quantize_mx(
-                out=wcodes[:, cols].bitcast(E4M3X4),
-                scales=wscales[:, cols],
-                in_=wgrp[:, cols, :].rearrange("p c j -> p (c j)"),
+
+        def prepare_w():
+            nc.vector.tensor_copy(
+                out=wgrp[:, 0:W_SPLIT, :].rearrange("p (c i) j -> p c j i", i=4),
+                in_=wraw[:, :, 0:W_SPLIT].rearrange("p j (c i) -> p c j i", i=4),
             )
+            nc.scalar.copy(
+                out=wgrp[:, W_SPLIT:D, :].rearrange("p (c i) j -> p c j i", i=4),
+                in_=wraw[:, :, W_SPLIT:D].rearrange("p j (c i) -> p c j i", i=4),
+            )
+            for n in range(D // N_TILE):
+                cols = slice(n * N_TILE, (n + 1) * N_TILE)
+                nc.vector.quantize_mx(
+                    out=wcodes[:, cols].bitcast(E4M3X4),
+                    scales=wscales[:, cols],
+                    in_=wgrp[:, cols, :].rearrange("p c j -> p (c j)"),
+                )
 
         gl_t = {}
         xt_t = {}
@@ -88,57 +94,54 @@ def tile_moelineara_t_kernel(tc, x, W, grad_out, out):
         code_t = {}
         stage_t = {}
 
-        def relay(i):
-            if i < 0 or i >= NG:
+        def relay(u):
+            if u < 0 or u >= NU:
                 return
-            c, t0 = where[i]
-            gl = ring.tile([P, GROUP * K], BF16, name="gl")
+            c, t0 = where[u]
+            gl = ring.tile([P, PAIR * K], BF16, name="gl")
             nc.vector.tensor_copy(
-                out=gl[:].rearrange("a (t e r) -> a t e r", t=GROUP, e=E),
-                in_=raw[c][:, :, t0 * R : (t0 + GROUP) * R].rearrange("a e (t r) -> a t e r", r=R),
+                out=gl[:].bitcast(F32).rearrange("a (t u e w) -> a t u e w", t=PAIR, u=2, e=E),
+                in_=raw_words[c][:, :, t0 : t0 + PAIR, :, :].rearrange("a e t w u -> a t u e w"),
             )
-            gl_t[i] = gl
+            gl_t[u] = gl
 
-        def transposes(i, h):
-            if i < 0 or i >= NG:
+        def transposes(u):
+            if u < 0 or u >= NU:
                 return
-            xt = tpsum.tile([P, 4, P], F32, name="xt")
-            words = gl_t[i][:].bitcast(F32).rearrange("a (t p u) -> a t u p", t=GROUP, u=2)
-            for tt in range(2):
-                for u in range(2):
-                    nc.tensor.transpose(xt[:, 2 * tt + u, :], words[:, 2 * h + tt, u, :], ident[:])
-            xt_t[(i, h)] = xt
+            xt = tpsum.tile([P, 2 * PAIR, P], F32, name="xt")
+            planes = gl_t[u][:].bitcast(F32).rearrange("a (q p) -> a q p", p=P)
+            for q in range(2 * PAIR):
+                nc.tensor.transpose(xt[:, q, :], planes[:, q, :], ident[:])
+            xt_t[u] = xt
 
-        def unload(i, h, on_scalar):
-            if i < 0 or i >= NG:
+        def unload(u):
+            if u < 0 or u >= NU:
                 return
-            if h == 0:
-                gq = ring.tile([P, GROUP * K], BF16, name="gq", align_bytes=64)
-                gq_t[i] = gq
-            dst = gq_t[i][:].bitcast(F32).rearrange("p (t a u) -> p t a u", t=GROUP, u=2)
-            src = xt_t[(i, h)][:].rearrange("p (t u) a -> p t a u", u=2)
-            if on_scalar:
-                nc.scalar.copy(out=dst[:, 2 * h : 2 * h + 2], in_=src)
+            gq = ring.tile([P, PAIR * K], BF16, name="gq", align_bytes=64)
+            dst = gq[:].bitcast(F32).rearrange("p (t a u) -> p t a u", t=PAIR, u=2)
+            src = xt_t[u][:].rearrange("p (t u) a -> p t a u", u=2)
+            if u < SCALAR_UNLOADS:
+                nc.scalar.copy(out=dst, in_=src)
             else:
-                nc.vector.tensor_copy(out=dst[:, 2 * h : 2 * h + 2], in_=src)
+                nc.vector.tensor_copy(out=dst, in_=src)
+            gq_t[u] = gq
 
-        def quantise(i):
-            if i < 0 or i >= NG:
+        def quantise(u):
+            if u < 0 or u >= NU:
                 return
-            codes = ring.tile([P, GROUP * P], U32, name="gcodes", align_bytes=64)
-            scales = ring.tile([P, GROUP * P], U8, name="gscales", align_bytes=64)
-            nc.vector.quantize_mx(out=codes[:].bitcast(E5M2X4), scales=scales[:], in_=gq_t[i][:])
-            code_t[i] = (codes, scales)
+            codes = ring.tile([P, PAIR * P], U32, name="gcodes", align_bytes=64)
+            scales = ring.tile([P, PAIR * P], U8, name="gscales", align_bytes=64)
+            nc.vector.quantize_mx(out=codes[:].bitcast(E5M2X4), scales=scales[:], in_=gq_t[u][:])
+            code_t[u] = (codes, scales)
 
-        def multiply(i, j_list):
-            if i < 0 or i >= NG:
+        def multiply(u, t):
+            if u < 0 or u >= NU:
                 return
-            codes, scales = code_t[i]
-            if i not in stage_t:
-                stage = stages.tile([P, GROUP, D], F32, name="stage")
-                stage_t[i] = stage
-            for j in j_list:
-                t, n = j // 2, j % 2
+            codes, scales = code_t[u]
+            if t == 0:
+                stage = stages.tile([P, PAIR, D], F32, name="stage")
+                stage_t[u] = stage
+            for n in range(D // N_TILE):
                 acc = apsum.tile([P, N_TILE], F32, name="acc")
                 nc.tensor.matmul_mx(
                     out=acc[:],
@@ -149,33 +152,28 @@ def tile_moelineara_t_kernel(tc, x, W, grad_out, out):
                     start=True,
                     stop=True,
                 )
-                dst = stage_t[i][:, t, n * N_TILE : (n + 1) * N_TILE]
-                if j in VECTOR_BANKS:
+                dst = stage_t[u][:, t, n * N_TILE : (n + 1) * N_TILE]
+                if t == 1 and n == 1:
                     nc.vector.tensor_copy(out=dst, in_=acc[:])
                 else:
                     nc.scalar.copy(out=dst, in_=acc[:])
+            if u < TILE_STORES:
+                store(u, t, t + 1)
+            elif t == PAIR - 1:
+                store(u, 0, PAIR)
 
-        def store(i, t0, t1):
-            if i < 0 or i >= NG:
-                return
+        def store(u, t0, t1):
             nc.sync.dma_start(
-                out=ov[:, (i * GROUP + t0) * D : (i * GROUP + t1) * D],
-                in_=stage_t[i][:, t0:t1, :].rearrange("p t d -> p (t d)"),
+                out=ov[:, (u * PAIR + t0) * D : (u * PAIR + t1) * D],
+                in_=stage_t[u][:, t0:t1, :].rearrange("p t d -> p (t d)"),
             )
 
-        relay(0)
-        for i in range(-2, NG):
-            unload(i + 1, 1, i < 0)
-            multiply(i, (0, 1, 2, 3))
-            if i < HALF_STORES:
-                store(i, 0, 2)
-            quantise(i + 1)
-            transposes(i + 2, 0)
-            unload(i + 2, 0, i < 0)
-            relay(i + 3)
-            multiply(i, (4, 5, 6, 7))
-            transposes(i + 2, 1)
-            if i < HALF_STORES:
-                store(i, 2, 4)
-            else:
-                store(i, 0, 4)
+        for s in range(-AHEAD_RELAY, NU):
+            multiply(s, 0)
+            relay(s + AHEAD_RELAY)
+            multiply(s, 1)
+            transposes(s + AHEAD_TRANSPOSE)
+            unload(s + AHEAD_UNLOAD)
+            quantise(s + AHEAD_QUANTISE)
+            if s == W_STEP:
+                prepare_w()

from contextlib import ExitStack

import concourse.mybir as mybir
from concourse.masks import make_identity

F32 = mybir.dt.float32
BF16 = mybir.dt.bfloat16
U32 = mybir.dt.uint32
U8 = mybir.dt.uint8
E4M3X4 = mybir.dt.float8_e4m3fn_x4
E5M2X4 = mybir.dt.float8_e5m2_x4

P = 128
E, R, D = 8, 64, 1024
K = E * R
TOKENS = 4096
NT = TOKENS // P
PAIR = 2
NU = NT // PAIR
N_TILE = 512
CHUNKS = (8, 8, 16)
W_SPLIT = 672
W_STEP = -2
SCALAR_UNLOADS = 2
TILE_STORES = 2
AHEAD_RELAY, AHEAD_TRANSPOSE, AHEAD_UNLOAD, AHEAD_QUANTISE = 5, 4, 3, 2
MANUAL = True

FLOPS = 2 * TOKENS * K * D
BYTES = TOKENS * K * 2 + K * D * 2 + TOKENS * D * 4


def tile_moelineara_t_kernel(tc, x, W, grad_out, out):
    nc = tc.nc
    gv = grad_out.rearrange("e b (c t) r -> (b c) e (t r)", t=NT)
    wv = W.rearrange("e (q j) d -> (e q) (j d)", j=4)
    ov = out.rearrange("b (c t) d -> (b c) (t d)", t=NT)

    with ExitStack() as ctx:
        keep = ctx.enter_context(tc.tile_pool(name="keep", bufs=1))
        ring = ctx.enter_context(tc.tile_pool(name="ring", bufs=3))
        stages = ctx.enter_context(tc.tile_pool(name="stages", bufs=NU))
        tpsum = ctx.enter_context(tc.psum_pool(name="tpsum", bufs=2))
        apsum = ctx.enter_context(tc.psum_pool(name="apsum", bufs=6))
        if MANUAL:
            ctx.enter_context(tc.manual_schedule())

        wraw = keep.tile([P, 4, D], BF16, name="wraw")
        raw_words = []
        where = []
        t_at = 0
        for c, n in enumerate(CHUNKS):
            chunk = keep.tile([P, E * n * R], BF16, name="raw%d" % c)
            by_expert = chunk[:].rearrange("a (e x) -> a e x", e=E)
            for h in range(2):
                nc.sync.dma_start(
                    out=by_expert[:, 4 * h : 4 * h + 4, :],
                    in_=gv[:, 4 * h : 4 * h + 4, t_at * R : (t_at + n) * R],
                )
            if c == 0:
                nc.sync.dma_start(out=wraw[:].rearrange("p j d -> p (j d)"), in_=wv)
            raw_words.append(chunk[:].bitcast(F32).rearrange("a (e t w u) -> a e t w u", e=E, w=R // 4, u=2))
            for t0 in range(0, n, PAIR):
                where.append((c, t0))
            t_at += n

        ident = keep.tile([P, P], F32, name="ident")
        make_identity(nc, ident[:])

        wgrp = keep.tile([P, D, 4], BF16, name="wgrp", align_bytes=64)
        wcodes = keep.tile([P, D], U32, name="wcodes", align_bytes=64)
        wscales = keep.tile([P, D], U8, name="wscales", align_bytes=64)

        def prepare_w():
            nc.vector.tensor_copy(
                out=wgrp[:, 0:W_SPLIT, :].rearrange("p (c i) j -> p c j i", i=4),
                in_=wraw[:, :, 0:W_SPLIT].rearrange("p j (c i) -> p c j i", i=4),
            )
            nc.scalar.copy(
                out=wgrp[:, W_SPLIT:D, :].rearrange("p (c i) j -> p c j i", i=4),
                in_=wraw[:, :, W_SPLIT:D].rearrange("p j (c i) -> p c j i", i=4),
            )
            for n in range(D // N_TILE):
                cols = slice(n * N_TILE, (n + 1) * N_TILE)
                nc.vector.quantize_mx(
                    out=wcodes[:, cols].bitcast(E4M3X4),
                    scales=wscales[:, cols],
                    in_=wgrp[:, cols, :].rearrange("p c j -> p (c j)"),
                )

        gl_t = {}
        xt_t = {}
        gq_t = {}
        code_t = {}
        stage_t = {}

        def relay(u):
            if u < 0 or u >= NU:
                return
            c, t0 = where[u]
            gl = ring.tile([P, PAIR * K], BF16, name="gl")
            nc.vector.tensor_copy(
                out=gl[:].bitcast(F32).rearrange("a (t u e w) -> a t u e w", t=PAIR, u=2, e=E),
                in_=raw_words[c][:, :, t0 : t0 + PAIR, :, :].rearrange("a e t w u -> a t u e w"),
            )
            gl_t[u] = gl

        def transposes(u):
            if u < 0 or u >= NU:
                return
            xt = tpsum.tile([P, 2 * PAIR, P], F32, name="xt")
            planes = gl_t[u][:].bitcast(F32).rearrange("a (q p) -> a q p", p=P)
            for q in range(2 * PAIR):
                nc.tensor.transpose(xt[:, q, :], planes[:, q, :], ident[:])
            xt_t[u] = xt

        def unload(u):
            if u < 0 or u >= NU:
                return
            gq = ring.tile([P, PAIR * K], BF16, name="gq", align_bytes=64)
            dst = gq[:].bitcast(F32).rearrange("p (t a u) -> p t a u", t=PAIR, u=2)
            src = xt_t[u][:].rearrange("p (t u) a -> p t a u", u=2)
            if u < SCALAR_UNLOADS:
                nc.scalar.copy(out=dst, in_=src)
            else:
                nc.vector.tensor_copy(out=dst, in_=src)
            gq_t[u] = gq

        def quantise(u):
            if u < 0 or u >= NU:
                return
            codes = ring.tile([P, PAIR * P], U32, name="gcodes", align_bytes=64)
            scales = ring.tile([P, PAIR * P], U8, name="gscales", align_bytes=64)
            nc.vector.quantize_mx(out=codes[:].bitcast(E5M2X4), scales=scales[:], in_=gq_t[u][:])
            code_t[u] = (codes, scales)

        def multiply(u, t):
            if u < 0 or u >= NU:
                return
            codes, scales = code_t[u]
            if t == 0:
                stage = stages.tile([P, PAIR, D], F32, name="stage")
                stage_t[u] = stage
            for n in range(D // N_TILE):
                acc = apsum.tile([P, N_TILE], F32, name="acc")
                nc.tensor.matmul_mx(
                    out=acc[:],
                    lhsT=codes[:, t * P : (t + 1) * P].bitcast(E5M2X4),
                    lhsT_scale=scales[:, t * P : (t + 1) * P],
                    rhs=wcodes[:, n * N_TILE : (n + 1) * N_TILE].bitcast(E4M3X4),
                    rhs_scale=wscales[:, n * N_TILE : (n + 1) * N_TILE],
                    start=True,
                    stop=True,
                )
                dst = stage_t[u][:, t, n * N_TILE : (n + 1) * N_TILE]
                if t == 1 and n == 1:
                    nc.vector.tensor_copy(out=dst, in_=acc[:])
                else:
                    nc.scalar.copy(out=dst, in_=acc[:])
            if u < TILE_STORES:
                store(u, t, t + 1)
            elif t == PAIR - 1:
                store(u, 0, PAIR)

        def store(u, t0, t1):
            nc.sync.dma_start(
                out=ov[:, (u * PAIR + t0) * D : (u * PAIR + t1) * D],
                in_=stage_t[u][:, t0:t1, :].rearrange("p t d -> p (t d)"),
            )

        for s in range(-AHEAD_RELAY, NU):
            multiply(s, 0)
            relay(s + AHEAD_RELAY)
            multiply(s, 1)
            transposes(s + AHEAD_TRANSPOSE)
            unload(s + AHEAD_UNLOAD)
            quantise(s + AHEAD_QUANTISE)
            if s == W_STEP:
                prepare_w()
